import numpy as np
import ml_dtypes


def mxq(x, axis, fmt="e4m3"):
    dtype, down = {"e4m3": (ml_dtypes.float8_e4m3fn, 7), "e5m2": (ml_dtypes.float8_e5m2, 14)}[fmt]
    v = np.moveaxis(np.asarray(x, np.float32).astype(ml_dtypes.bfloat16).astype(np.float64), axis, -1)
    blocks = v.reshape(v.shape[:-1] + (-1, 32))
    amax = np.abs(blocks).max(-1, keepdims=True)
    byte = np.maximum(np.where(amax > 0, np.frexp(amax)[1] - 1 + 127, 0) - down, 1)
    scale = np.exp2(byte - 127.0)
    codes = (blocks / scale).astype(np.float32).astype(dtype).astype(np.float64)
    return np.moveaxis((codes * scale).reshape(v.shape), -1, axis)


WIDE = False


def mx_kscale(k):
    if not WIDE:
        return np.ones(k)
    levels = np.array([10, -10, 5, -5, 0])
    if k % 512:
        return np.exp2(np.random.permutation(np.resize(levels, k // 32))).repeat(32)
    a = np.empty((k // 512, 16))
    for p in range(k // 512):
        a[p, :8] = np.random.permutation(np.resize(levels, 8))
        for g in range(8):
            far = levels[np.abs(levels - a[p, g]) >= 10]
            a[p, g + 8] = far[np.random.randint(len(far))]
    return np.exp2(a.ravel()).repeat(32)


BF16 = ml_dtypes.bfloat16


def bf(x):
    return np.asarray(x, np.float32).astype(BF16)


def f64(x):
    return np.asarray(x).astype(np.float64)


B, SS, SM, SL, N, D = 1, 512, 1024, 1536, 512, 512
T = SS + SM + SL
EPS = 1e-5


def setup_inputs():
    s = mx_kscale(N)
    d = {"x": bf(np.random.standard_normal((B, T, N))),
         "gamma": bf((1.0 + 0.1 * np.random.standard_normal(N)) * s),
         "beta": bf(0.1 * np.random.standard_normal(N) * s)}
    for c in ("s", "m", "l"):
        d["Wqkv_" + c] = bf(np.random.standard_normal((N, 3 * D)) * 1.5 / np.sqrt(N) / s[:, None])
        d["bqkv_" + c] = bf(0.1 * np.random.standard_normal(3 * D))
    return d


def layer_norm(x, gamma, beta):
    mu = x.mean(-1, keepdims=True)
    var = np.square(x - mu).mean(-1, keepdims=True)
    return (x - mu) / np.sqrt(var + EPS) * gamma + beta


def proj(hseg, W, b):
    return (mxq(hseg, 2, "e4m3") @ mxq(f64(W), 0, "e4m3")) + f64(b)


def reference(x, gamma, beta, Wqkv_s, bqkv_s, Wqkv_m, bqkv_m, Wqkv_l, bqkv_l):
    h = layer_norm(f64(x), f64(gamma), f64(beta))
    qkv_s = proj(h[:, :SS], Wqkv_s, bqkv_s)
    qkv_m = proj(h[:, SS:SS + SM], Wqkv_m, bqkv_m)
    qkv_l = proj(h[:, SS + SM:T], Wqkv_l, bqkv_l)
    return np.concatenate([qkv_s, qkv_m, qkv_l], axis=1)

@@ -1,0 +1,251 @@
+from contextlib import ExitStack
+
+import concourse.mybir as mybir
+from concourse.masks import make_identity
+
+F32 = mybir.dt.float32
+BF16 = mybir.dt.bfloat16
+I32 = mybir.dt.int32
+U32 = mybir.dt.uint32
+U8 = mybir.dt.uint8
+FP8X4 = mybir.dt.float8_e4m3fn_x4
+ACT = mybir.ActivationFunctionType
+ALU = mybir.AluOpType
+
+P = 128
+PACK = 4
+FEATURES = P * PACK
+OUT_COLS = 1536
+N_TILE = 512
+PIECES = OUT_COLS // N_TILE
+SEGMENT_TOKENS = (512, 1024, 1536)
+EPS = 1e-5
+GROUP = 2
+GROUP_TOKENS = GROUP * P
+CHUNKS_PER_BANK = N_TILE // GROUP_TOKENS
+RUN = 4
+
+FLOPS = 2 * sum(SEGMENT_TOKENS) * FEATURES * OUT_COLS
+
+
+def tile_multiscalesattn_pa_kernel(
+    tc, x, gamma, beta, Wqkv_s, bqkv_s, Wqkv_m, bqkv_m, Wqkv_l, bqkv_l, out
+):
+    nc = tc.nc
+    weights = (Wqkv_s, Wqkv_m, Wqkv_l)
+    biases = (bqkv_s, bqkv_m, bqkv_l)
+    n_scales = len(weights)
+
+    x_groups = x.flatten_outer_dims().rearrange("(g p i) k -> g p i k", p=P, i=GROUP)
+    out_groups = out.flatten_outer_dims().rearrange("(g p i) n -> g p i n", p=P, i=GROUP)
+    n_groups = sum(SEGMENT_TOKENS) // GROUP_TOKENS
+    first_group = [sum(SEGMENT_TOKENS[:c]) // GROUP_TOKENS for c in range(n_scales)]
+    scale_of_group = [max(c for c in range(n_scales) if first_group[c] <= g) for g in range(n_groups)]
+
+    with ExitStack() as ctx:
+        ctx.enter_context(tc.manual_schedule())
+        consts = ctx.enter_context(tc.tile_pool(name="consts", bufs=1))
+        small = ctx.enter_context(tc.tile_pool(name="small", bufs=4))
+        scratch = ctx.enter_context(tc.tile_pool(name="scratch", bufs=4))
+        work = ctx.enter_context(tc.tile_pool(name="work", bufs=3))
+        results = ctx.enter_context(tc.tile_pool(name="results", bufs=6))
+        psum_t = ctx.enter_context(tc.psum_pool(name="psum_t", bufs=4))
+        psum_acc = ctx.enter_context(tc.psum_pool(name="psum_acc", bufs=4))
+
+        gamma_raw = consts.tile([P, PACK], BF16)
+        beta_raw = consts.tile([P, PACK], BF16)
+        nc.sync.dma_start(out=gamma_raw[:], in_=gamma.rearrange("(p j) -> p j", j=PACK))
+        nc.sync.dma_start(out=beta_raw[:], in_=beta.rearrange("(p j) -> p j", j=PACK))
+        bias_src = consts.tile([P, n_scales * OUT_COLS], BF16)
+        nc.vector.memset(bias_src[:].bitcast(I32), 0)
+        for c in range(n_scales):
+            nc.scalar.dma_start(
+                out=bias_src[0:1, c * OUT_COLS : (c + 1) * OUT_COLS],
+                in_=biases[c].rearrange("(o n) -> o n", o=1),
+            )
+
+        x_all = consts.tile([P, n_groups, GROUP, FEATURES], BF16)
+        w_raw = [consts.tile([P, PACK, OUT_COLS], BF16, name="w_raw%d" % c) for c in range(n_scales)]
+        for g in range(n_groups):
+            nc.sync.dma_start(out=x_all[:, g, :, :], in_=x_groups[g])
+            c = scale_of_group[g]
+            if g == first_group[c] + 1:
+                nc.sync.dma_start(out=w_raw[c][:], in_=weights[c].rearrange("(p j) n -> p j n", j=PACK))
+
+        identity = consts.tile([P, P], F32)
+        make_identity(nc, identity[:])
+        eps = consts.tile([P, 1], F32)
+        nc.vector.memset(eps[:], EPS)
+        ones = consts.tile([P, P], BF16)
+        nc.vector.memset(ones[:], 1.0)
+
+        gb_cols = consts.tile([P, 2 * PACK], F32)
+        nc.vector.tensor_copy(out=gb_cols[:, 0:PACK], in_=gamma_raw[:])
+        nc.vector.tensor_copy(out=gb_cols[:, PACK : 2 * PACK], in_=beta_raw[:])
+
+        bias_rows = consts.tile([P, n_scales * OUT_COLS], BF16)
+
+        def spread_bias(piece):
+            cols = slice(piece * N_TILE, (piece + 1) * N_TILE)
+            bias_bank = psum_acc.tile([P, N_TILE], BF16, tag="acc")
+            nc.tensor.matmul(out=bias_bank[:], lhsT=ones[:], rhs=bias_src[:, cols], start=True, stop=True)
+            nc.vector.tensor_copy(out=bias_rows[:, cols], in_=bias_bank[:])
+
+        w_codes = [consts.tile([P, OUT_COLS], U32, name="w_codes%d" % c, align_bytes=64) for c in range(n_scales)]
+        w_scales = [consts.tile([P, OUT_COLS], U8, name="w_scales%d" % c, align_bytes=64) for c in range(n_scales)]
+        w_grouped = {}
+
+        def regroup_weights(piece, engine):
+            c, n = divmod(piece, PIECES)
+            w_grouped[piece] = work.tile([P, N_TILE, PACK], BF16, name="w_grouped", align_bytes=64)
+            dst = w_grouped[piece][:]
+            src = w_raw[c][:, :, n * N_TILE : (n + 1) * N_TILE]
+            if engine == "gpsimd":
+                nc.gpsimd.tensor_scalar(
+                    out=dst, in0=src.rearrange("p j w -> p w j"), scalar1=1.0, scalar2=0.0, op0=ALU.mult, op1=ALU.add
+                )
+            else:
+                dst_runs = dst.rearrange("p (w r) j -> p w j r", r=RUN)
+                src_runs = src.rearrange("p j (w r) -> p w j r", r=RUN)
+                if engine == "vector":
+                    nc.vector.tensor_copy(out=dst_runs, in_=src_runs)
+                else:
+                    nc.scalar.copy(out=dst_runs, in_=src_runs)
+
+        def quantise_weights(piece):
+            c, n = divmod(piece, PIECES)
+            cols = slice(n * N_TILE, (n + 1) * N_TILE)
+            nc.vector.quantize_mx(
+                out=w_codes[c][:, cols].bitcast(FP8X4),
+                scales=w_scales[c][:, cols],
+                in_=w_grouped[piece][:].rearrange("p w j -> p (w j)"),
+            )
+
+        neg_mean = {}
+        std = {}
+        rstd = {}
+        xT = {}
+        hT = {}
+        h_grouped = {}
+        h_codes = {}
+        h_scales = {}
+
+        def statistics(g):
+            neg_mean[g] = small.tile([P, GROUP], F32, name="neg_mean")
+            sum_sq = small.tile([P, GROUP], F32)
+            for i in range(GROUP):
+                unread = scratch.tile([P, FEATURES], BF16)
+                nc.scalar.activation(
+                    out=unread[:], in_=x_all[:, g, i, :], func=ACT.Copy, scale=-1.0 / FEATURES,
+                    accum_out=neg_mean[g][:, i : i + 1],
+                )
+            for i in range(GROUP):
+                unread = scratch.tile([P, FEATURES], BF16)
+                nc.scalar.activation(
+                    out=unread[:], in_=x_all[:, g, i, :], func=ACT.Square,
+                    bias=neg_mean[g][:, i : i + 1], scale=1.0, accum_out=sum_sq[:, i : i + 1],
+                )
+            std[g] = small.tile([P, GROUP], F32, name="std")
+            nc.scalar.activation(out=std[g][:], in_=sum_sq[:], func=ACT.Sqrt, bias=eps[:, 0:1], scale=1.0 / FEATURES)
+
+        def reciprocal(g):
+            rstd[g] = small.tile([P, GROUP], F32, name="rstd")
+            nc.vector.reciprocal(out=rstd[g][:], in_=std[g][:])
+
+        def normalise_and_transpose(g):
+            xn = work.tile([P, GROUP, FEATURES], F32)
+            for i in range(GROUP):
+                nc.gpsimd.tensor_scalar(
+                    out=xn[:, i, :].rearrange("p (j q) -> p j q", j=PACK),
+                    in0=x_all[:, g, i, :].rearrange("p (q j) -> p j q", j=PACK),
+                    scalar1=neg_mean[g][:, i : i + 1], scalar2=rstd[g][:, i : i + 1],
+                    op0=ALU.add, op1=ALU.mult,
+                )
+            xT[g] = []
+            for b in range(PACK // CHUNKS_PER_BANK):
+                bank = psum_t.tile([P, CHUNKS_PER_BANK, GROUP_TOKENS], F32, name="xT", tag="xT")
+                xT[g].append(bank)
+                for jj in range(CHUNKS_PER_BANK):
+                    j = b * CHUNKS_PER_BANK + jj
+                    for i in range(GROUP):
+                        nc.tensor.transpose(
+                            out=bank[:, jj, i * P : (i + 1) * P],
+                            in_=xn[:, i, j * P : (j + 1) * P],
+                            identity=identity[:],
+                        )
+
+        def scale_and_shift(g):
+            hT[g] = work.tile([P, PACK, GROUP_TOKENS], BF16, name="hT")
+            for j in range(PACK):
+                nc.scalar.activation(
+                    out=hT[g][:, j, :], in_=xT[g][j // CHUNKS_PER_BANK][:, j % CHUNKS_PER_BANK, :],
+                    func=ACT.Identity, scale=gb_cols[:, j : j + 1], bias=gb_cols[:, PACK + j : PACK + j + 1],
+                )
+
+        def regroup(g):
+            h_grouped[g] = work.tile([P, GROUP_TOKENS, PACK], BF16, name="h_grouped", align_bytes=64)
+            nc.gpsimd.tensor_scalar(
+                out=h_grouped[g][:], in0=hT[g][:].rearrange("p j w -> p w j"),
+                scalar1=1.0, scalar2=0.0, op0=ALU.mult, op1=ALU.add,
+            )
+
+        def quantise(g):
+            h_codes[g] = work.tile([P, GROUP_TOKENS], U32, name="h_codes", align_bytes=64)
+            h_scales[g] = work.tile([P, GROUP_TOKENS], U8, name="h_scales", align_bytes=64)
+            nc.vector.quantize_mx(
+                out=h_codes[g][:].bitcast(FP8X4), scales=h_scales[g][:],
+                in_=h_grouped[g][:].rearrange("p w j -> p (w j)"),
+            )
+
+        def project(g, i):
+            c = scale_of_group[g]
+            tokens = slice(i * P, (i + 1) * P)
+            result = results.tile([P, OUT_COLS], F32)
+            for n in range(PIECES):
+                cols = slice(n * N_TILE, (n + 1) * N_TILE)
+                acc = psum_acc.tile([P, N_TILE], F32, tag="acc")
+                nc.tensor.matmul_mx(
+                    out=acc[:],
+                    lhsT=h_codes[g][:, tokens].bitcast(FP8X4), lhsT_scale=h_scales[g][:, tokens],
+                    rhs=w_codes[c][:, cols].bitcast(FP8X4), rhs_scale=w_scales[c][:, cols],
+                    start=True, stop=True,
+                )
+                nc.vector.tensor_tensor(
+                    out=result[:, cols], in0=acc[:],
+                    in1=bias_rows[:, c * OUT_COLS + n * N_TILE : c * OUT_COLS + (n + 1) * N_TILE], op=ALU.add,
+                )
+            nc.sync.dma_start(out=out_groups[g, :, i, :], in_=result[:])
+
+        n_pieces = n_scales * PIECES
+        regroup_step = [1 if piece < PIECES else 2 + (piece - PIECES) // 2 for piece in range(n_pieces)]
+
+        def in_range(g):
+            return 0 <= g < n_groups
+
+        for step in range(n_groups + 4):
+            if in_range(step - 1):
+                reciprocal(step - 1)
+            if in_range(step - 3):
+                quantise(step - 3)
+            if in_range(step - 4):
+                project(step - 4, 1)
+            if in_range(step - 3):
+                project(step - 3, 0)
+            for piece in range(n_pieces):
+                if regroup_step[piece] == step - 1:
+                    quantise_weights(piece)
+                    spread_bias(piece)
+            if in_range(step - 2):
+                scale_and_shift(step - 2)
+            if in_range(step):
+                statistics(step)
+            if in_range(step - 1):
+                normalise_and_transpose(step - 1)
+            if in_range(step - 2):
+                regroup(step - 2)
+            for piece in range(n_pieces):
+                if regroup_step[piece] == step:
+                    if piece < PIECES:
+                        regroup_weights(piece, "vector")
+                    else:
+                        regroup_weights(piece, "scalar" if piece % 2 == 1 else "gpsimd")

@@ -24,6 +24,7 @@ GROUP = 2
 GROUP_TOKENS = GROUP * P
 CHUNKS_PER_BANK = N_TILE // GROUP_TOKENS
 RUN = 4
+VECTOR_STATS = 5
 
 FLOPS = 2 * sum(SEGMENT_TOKENS) * FEATURES * OUT_COLS
 
@@ -45,61 +46,89 @@ def tile_multiscalesattn_pa_kernel(
     with ExitStack() as ctx:
         ctx.enter_context(tc.manual_schedule())
         consts = ctx.enter_context(tc.tile_pool(name="consts", bufs=1))
-        small = ctx.enter_context(tc.tile_pool(name="small", bufs=4))
-        scratch = ctx.enter_context(tc.tile_pool(name="scratch", bufs=4))
-        work = ctx.enter_context(tc.tile_pool(name="work", bufs=3))
-        results = ctx.enter_context(tc.tile_pool(name="results", bufs=6))
+        small = ctx.enter_context(tc.tile_pool(name="small", bufs=8))
+        scratch = ctx.enter_context(tc.tile_pool(name="scratch", bufs=2))
+        work = ctx.enter_context(tc.tile_pool(name="work", bufs=4))
+        results = ctx.enter_context(tc.tile_pool(name="results", bufs=8))
         psum_t = ctx.enter_context(tc.psum_pool(name="psum_t", bufs=4))
         psum_acc = ctx.enter_context(tc.psum_pool(name="psum_acc", bufs=4))
 
-        gamma_raw = consts.tile([P, PACK], BF16)
-        beta_raw = consts.tile([P, PACK], BF16)
-        nc.sync.dma_start(out=gamma_raw[:], in_=gamma.rearrange("(p j) -> p j", j=PACK))
-        nc.sync.dma_start(out=beta_raw[:], in_=beta.rearrange("(p j) -> p j", j=PACK))
-        bias_src = consts.tile([P, n_scales * OUT_COLS], BF16)
+        bias_src = consts.tile([P, OUT_COLS], BF16)
         nc.vector.memset(bias_src[:].bitcast(I32), 0)
-        for c in range(n_scales):
-            nc.scalar.dma_start(
-                out=bias_src[0:1, c * OUT_COLS : (c + 1) * OUT_COLS],
-                in_=biases[c].rearrange("(o n) -> o n", o=1),
-            )
-
-        x_all = consts.tile([P, n_groups, GROUP, FEATURES], BF16)
-        w_raw = [consts.tile([P, PACK, OUT_COLS], BF16, name="w_raw%d" % c) for c in range(n_scales)]
-        for g in range(n_groups):
-            nc.sync.dma_start(out=x_all[:, g, :, :], in_=x_groups[g])
-            c = scale_of_group[g]
-            if g == first_group[c] + 1:
-                nc.sync.dma_start(out=w_raw[c][:], in_=weights[c].rearrange("(p j) n -> p j n", j=PACK))
-
-        identity = consts.tile([P, P], F32)
-        make_identity(nc, identity[:])
         eps = consts.tile([P, 1], F32)
         nc.vector.memset(eps[:], EPS)
-        ones = consts.tile([P, P], BF16)
-        nc.vector.memset(ones[:], 1.0)
+        root_eps = consts.tile([P, 1], F32)
+        nc.scalar.activation(out=root_eps[:], in_=eps[:], func=ACT.Sqrt)
+        identity = consts.tile([P, P], F32)
+        make_identity(nc, identity[:])
+        identity_bf16 = consts.tile([P, P], BF16)
+        nc.gpsimd.tensor_copy(out=identity_bf16[:], in_=identity[:])
+
+        x_all = consts.tile([P, n_groups, GROUP, FEATURES], BF16)
+        w_raw = [
+            [consts.tile([P, PACK, N_TILE], BF16, name="w_raw%d_%d" % (c, n)) for n in range(PIECES)]
+            for c in range(n_scales)
+        ]
+
+        def load_x(first, last):
+            nc.sync.dma_start(
+                out=x_all[:, first : last + 1, :, :], in_=x_groups[first : last + 1].rearrange("g p i k -> p g i k")
+            )
+
+        def load_weights(piece):
+            c, n = divmod(piece, PIECES)
+            rows = weights[c].rearrange("(p j) n -> p j n", j=PACK)
+            nc.sync.dma_start(out=w_raw[c][n][:], in_=rows[:, :, n * N_TILE : (n + 1) * N_TILE])
+
+        gamma_raw = consts.tile([P, PACK], BF16)
+        beta_raw = consts.tile([P, PACK], BF16)
+
+        load_x(0, 0)
+        for c in range(n_scales):
+            nc.sync.dma_start(out=bias_src[c : c + 1, :], in_=biases[c].rearrange("(o n) -> o n", o=1))
+        load_weights(0)
+        load_x(1, 1)
+        nc.sync.dma_start(out=gamma_raw[:], in_=gamma.rearrange("(p j) -> p j", j=PACK))
+        nc.sync.dma_start(out=beta_raw[:], in_=beta.rearrange("(p j) -> p j", j=PACK))
+        load_weights(1)
+        load_x(2, 2)
+        load_weights(2)
+        load_x(3, 3)
+        load_weights(3)
+        load_weights(4)
+        load_weights(5)
+        load_x(4, 5)
+        for piece in range(6, 9):
+            load_weights(piece)
+        for first in range(6, n_groups, 2):
+            load_x(first, first + 1)
 
         gb_cols = consts.tile([P, 2 * PACK], F32)
-        nc.vector.tensor_copy(out=gb_cols[:, 0:PACK], in_=gamma_raw[:])
-        nc.vector.tensor_copy(out=gb_cols[:, PACK : 2 * PACK], in_=beta_raw[:])
+        nc.gpsimd.tensor_copy(out=gb_cols[:, 0:PACK], in_=gamma_raw[:])
+        nc.gpsimd.tensor_copy(out=gb_cols[:, PACK : 2 * PACK], in_=beta_raw[:])
 
         bias_rows = consts.tile([P, n_scales * OUT_COLS], BF16)
 
         def spread_bias(piece):
-            cols = slice(piece * N_TILE, (piece + 1) * N_TILE)
+            c, n = divmod(piece, PIECES)
             bias_bank = psum_acc.tile([P, N_TILE], BF16, tag="acc")
-            nc.tensor.matmul(out=bias_bank[:], lhsT=ones[:], rhs=bias_src[:, cols], start=True, stop=True)
-            nc.vector.tensor_copy(out=bias_rows[:, cols], in_=bias_bank[:])
+            nc.tensor.matmul(
+                out=bias_bank[:], lhsT=identity_bf16[:, c : c + 1].to_broadcast([P, P]),
+                rhs=bias_src[:, n * N_TILE : (n + 1) * N_TILE], start=True, stop=True,
+            )
+            nc.scalar.copy(out=bias_rows[:, piece * N_TILE : (piece + 1) * N_TILE], in_=bias_bank[:])
 
         w_codes = [consts.tile([P, OUT_COLS], U32, name="w_codes%d" % c, align_bytes=64) for c in range(n_scales)]
         w_scales = [consts.tile([P, OUT_COLS], U8, name="w_scales%d" % c, align_bytes=64) for c in range(n_scales)]
         w_grouped = {}
 
-        def regroup_weights(piece, engine):
+        def regroup_weights(piece, engine, part, parts):
             c, n = divmod(piece, PIECES)
-            w_grouped[piece] = work.tile([P, N_TILE, PACK], BF16, name="w_grouped", align_bytes=64)
-            dst = w_grouped[piece][:]
-            src = w_raw[c][:, :, n * N_TILE : (n + 1) * N_TILE]
+            if part == 0:
+                w_grouped[piece] = work.tile([P, N_TILE, PACK], BF16, name="w_grouped", align_bytes=64)
+            cols = slice(part * N_TILE // parts, (part + 1) * N_TILE // parts)
+            dst = w_grouped[piece][:, cols, :]
+            src = w_raw[c][n][:, :, cols]
             if engine == "gpsimd":
                 nc.gpsimd.tensor_scalar(
                     out=dst, in0=src.rearrange("p j w -> p w j"), scalar1=1.0, scalar2=0.0, op0=ALU.mult, op1=ALU.add
@@ -121,6 +150,7 @@ def tile_multiscalesattn_pa_kernel(
                 in_=w_grouped[piece][:].rearrange("p w j -> p (w j)"),
             )
 
+        moments_of = {}
         neg_mean = {}
         std = {}
         rstd = {}
@@ -130,7 +160,23 @@ def tile_multiscalesattn_pa_kernel(
         h_codes = {}
         h_scales = {}
 
-        def statistics(g):
+        def vector_statistics(g):
+            moments = small.tile([P, GROUP, 2], F32)
+            partial = small.tile([P, GROUP, 6], F32)
+            for i in range(GROUP):
+                nc.vector.bn_stats(out=partial[:, i, :], in_=x_all[:, g, i, :])
+            for i in range(GROUP):
+                nc.vector.bn_aggr(out=moments[:, i, :], in_=partial[:, i, :])
+            moments_of[g] = moments
+
+        def roots(g):
+            moments = moments_of[g]
+            neg_mean[g] = small.tile([P, GROUP], F32, name="neg_mean")
+            nc.scalar.activation(out=neg_mean[g][:], in_=moments[:, :, 0], func=ACT.Copy, scale=-1.0)
+            std[g] = small.tile([P, GROUP], F32, name="std")
+            nc.scalar.activation(out=std[g][:], in_=moments[:, :, 1], func=ACT.Sqrt, bias=eps[:, 0:1], scale=1.0)
+
+        def scalar_statistics(g):
             neg_mean[g] = small.tile([P, GROUP], F32, name="neg_mean")
             sum_sq = small.tile([P, GROUP], F32)
             for i in range(GROUP):
@@ -214,38 +260,64 @@ def tile_multiscalesattn_pa_kernel(
                     out=result[:, cols], in0=acc[:],
                     in1=bias_rows[:, c * OUT_COLS + n * N_TILE : c * OUT_COLS + (n + 1) * N_TILE], op=ALU.add,
                 )
-            nc.sync.dma_start(out=out_groups[g, :, i, :], in_=result[:])
+                if g == n_groups - 1 and i == GROUP - 1:
+                    nc.sync.dma_start(out=out_groups[g, :, i, cols], in_=result[:, cols])
+            if g < n_groups - 1 or i < GROUP - 1:
+                nc.sync.dma_start(out=out_groups[g, :, i, :], in_=result[:])
 
-        n_pieces = n_scales * PIECES
-        regroup_step = [1 if piece < PIECES else 2 + (piece - PIECES) // 2 for piece in range(n_pieces)]
+        regroup_plan = {
+            -4: ((0, "vector"),), -3: ((1, "scalar"),), -2: ((2, "scalar"),), -1: ((3, "vector"), (4, "scalar")),
+            0: ((5, "scalar"),), 1: ((6, "scalar"),), 2: ((7, "gpsimd"),), 3: ((8, "scalar"),),
+        }
 
         def in_range(g):
             return 0 <= g < n_groups
 
-        for step in range(n_groups + 4):
-            if in_range(step - 1):
-                reciprocal(step - 1)
-            if in_range(step - 3):
-                quantise(step - 3)
-            if in_range(step - 4):
-                project(step - 4, 1)
-            if in_range(step - 3):
-                project(step - 3, 0)
-            for piece in range(n_pieces):
-                if regroup_step[piece] == step - 1:
-                    quantise_weights(piece)
+        gpsimd_parts = []
+        to_quantise = []
+        for s in range(-4, n_groups + 1):
+            pieces = regroup_plan.get(s, ())
+            if s + 4 < VECTOR_STATS:
+                vector_statistics(s + 4)
+            if s == -4:
+                for piece in range(n_scales * PIECES):
                     spread_bias(piece)
-            if in_range(step - 2):
-                scale_and_shift(step - 2)
-            if in_range(step):
-                statistics(step)
-            if in_range(step - 1):
-                normalise_and_transpose(step - 1)
-            if in_range(step - 2):
-                regroup(step - 2)
-            for piece in range(n_pieces):
-                if regroup_step[piece] == step:
-                    if piece < PIECES:
-                        regroup_weights(piece, "vector")
-                    else:
-                        regroup_weights(piece, "scalar" if piece % 2 == 1 else "gpsimd")
+            if s + 4 < VECTOR_STATS:
+                roots(s + 4)
+            for piece, engine in pieces:
+                if engine == "vector":
+                    regroup_weights(piece, engine, 0, 1)
+            if in_range(s + 3):
+                reciprocal(s + 3)
+            if in_range(s):
+                quantise(s)
+            if in_range(s - 1):
+                project(s - 1, 1)
+            if in_range(s):
+                project(s, 0)
+            for piece in to_quantise:
+                quantise_weights(piece)
+            to_quantise = [piece for piece, engine in pieces if engine != "gpsimd"]
+
+            scalar_pieces = [piece for piece, engine in pieces if engine == "scalar"]
+            if in_range(s + 2):
+                scale_and_shift(s + 2)
+            for piece in scalar_pieces:
+                regroup_weights(piece, "scalar", 0, 2)
+            if VECTOR_STATS <= s + 4 < n_groups:
+                scalar_statistics(s + 4)
+            for piece in scalar_pieces:
+                regroup_weights(piece, "scalar", 1, 2)
+
+            if in_range(s + 1):
+                regroup(s + 1)
+            gpsimd_parts += [(piece, part) for piece, engine in pieces if engine == "gpsimd" for part in range(4)]
+            for k in range(2):
+                if gpsimd_parts:
+                    piece, part = gpsimd_parts[0]
+                    gpsimd_parts = gpsimd_parts[1:]
+                    regroup_weights(piece, "gpsimd", part, 4)
+                    if part == 3:
+                        to_quantise.append(piece)
+                if k == 0 and in_range(s + 3):
+                    normalise_and_transpose(s + 3)

@@ -58,7 +58,7 @@ def tile_multiscalesattn_pa_kernel(
         eps = consts.tile([P, 1], F32)
         nc.vector.memset(eps[:], EPS)
         root_eps = consts.tile([P, 1], F32)
-        nc.scalar.activation(out=root_eps[:], in_=eps[:], func=ACT.Sqrt)
+        nc.scalar.activation(out=root_eps[:], in_=eps[:], func=ACT.Abs_reciprocal_sqrt)
         identity = consts.tile([P, P], F32)
         make_identity(nc, identity[:])
         identity_bf16 = consts.tile([P, P], BF16)
@@ -129,7 +129,17 @@ def tile_multiscalesattn_pa_kernel(
             cols = slice(part * N_TILE // parts, (part + 1) * N_TILE // parts)
             dst = w_grouped[piece][:, cols, :]
             src = w_raw[c][n][:, :, cols]
-            if engine == "gpsimd":
+            if engine == "tensor":
+                bank = psum_t.tile([P, 2 * N_TILE], BF16, name="xT", tag="xT")
+                width = N_TILE // PACK
+                for half in range(2):
+                    nc.tensor.matmul(
+                        out=bank[:, half * N_TILE : (half + 1) * N_TILE], lhsT=identity_bf16[:],
+                        rhs=src[:, :, half * width : (half + 1) * width].rearrange("p j w -> p w j"),
+                        start=True, stop=True,
+                    )
+                nc.scalar.copy(out=dst.rearrange("p w j -> p (w j)"), in_=bank[:])
+            elif engine == "gpsimd":
                 nc.gpsimd.tensor_scalar(
                     out=dst, in0=src.rearrange("p j w -> p w j"), scalar1=1.0, scalar2=0.0, op0=ALU.mult, op1=ALU.add
                 )
@@ -152,7 +162,6 @@ def tile_multiscalesattn_pa_kernel(
 
         moments_of = {}
         neg_mean = {}
-        std = {}
         rstd = {}
         xT = {}
         hT = {}
@@ -173,8 +182,10 @@ def tile_multiscalesattn_pa_kernel(
             moments = moments_of[g]
             neg_mean[g] = small.tile([P, GROUP], F32, name="neg_mean")
             nc.scalar.activation(out=neg_mean[g][:], in_=moments[:, :, 0], func=ACT.Copy, scale=-1.0)
-            std[g] = small.tile([P, GROUP], F32, name="std")
-            nc.scalar.activation(out=std[g][:], in_=moments[:, :, 1], func=ACT.Sqrt, bias=eps[:, 0:1], scale=1.0)
+            rstd[g] = small.tile([P, GROUP], F32, name="rstd")
+            nc.scalar.activation(
+                out=rstd[g][:], in_=moments[:, :, 1], func=ACT.Abs_reciprocal_sqrt, bias=eps[:, 0:1], scale=1.0
+            )
 
         def scalar_statistics(g):
             neg_mean[g] = small.tile([P, GROUP], F32, name="neg_mean")
@@ -191,12 +202,10 @@ def tile_multiscalesattn_pa_kernel(
                     out=unread[:], in_=x_all[:, g, i, :], func=ACT.Square,
                     bias=neg_mean[g][:, i : i + 1], scale=1.0, accum_out=sum_sq[:, i : i + 1],
                 )
-            std[g] = small.tile([P, GROUP], F32, name="std")
-            nc.scalar.activation(out=std[g][:], in_=sum_sq[:], func=ACT.Sqrt, bias=eps[:, 0:1], scale=1.0 / FEATURES)
-
-        def reciprocal(g):
             rstd[g] = small.tile([P, GROUP], F32, name="rstd")
-            nc.vector.reciprocal(out=rstd[g][:], in_=std[g][:])
+            nc.scalar.activation(
+                out=rstd[g][:], in_=sum_sq[:], func=ACT.Abs_reciprocal_sqrt, bias=eps[:, 0:1], scale=1.0 / FEATURES
+            )
 
         def normalise_and_transpose(g):
             xn = work.tile([P, GROUP, FEATURES], F32)
@@ -266,8 +275,8 @@ def tile_multiscalesattn_pa_kernel(
                 nc.sync.dma_start(out=out_groups[g, :, i, :], in_=result[:])
 
         regroup_plan = {
-            -4: ((0, "vector"),), -3: ((1, "scalar"),), -2: ((2, "scalar"),), -1: ((3, "vector"), (4, "scalar")),
-            0: ((5, "scalar"),), 1: ((6, "scalar"),), 2: ((7, "gpsimd"),), 3: ((8, "scalar"),),
+            -4: ((0, "vector"),), -3: ((1, "tensor"),), -2: ((2, "tensor"),), -1: ((3, "vector"), (4, "tensor")),
+            0: ((5, "tensor"),), 1: ((6, "scalar"),), 2: ((7, "gpsimd"),), 3: ((8, "scalar"),),
         }
 
         def in_range(g):
@@ -280,15 +289,16 @@ def tile_multiscalesattn_pa_kernel(
             if s + 4 < VECTOR_STATS:
                 vector_statistics(s + 4)
             if s == -4:
-                for piece in range(n_scales * PIECES):
+                for piece in range(PIECES):
                     spread_bias(piece)
             if s + 4 < VECTOR_STATS:
                 roots(s + 4)
+            if s == -4:
+                for piece in range(PIECES, n_scales * PIECES):
+                    spread_bias(piece)
             for piece, engine in pieces:
                 if engine == "vector":
                     regroup_weights(piece, engine, 0, 1)
-            if in_range(s + 3):
-                reciprocal(s + 3)
             if in_range(s):
                 quantise(s)
             if in_range(s - 1):
@@ -299,15 +309,15 @@ def tile_multiscalesattn_pa_kernel(
                 quantise_weights(piece)
             to_quantise = [piece for piece, engine in pieces if engine != "gpsimd"]
 
-            scalar_pieces = [piece for piece, engine in pieces if engine == "scalar"]
+            scalar_pieces = [(piece, engine) for piece, engine in pieces if engine in ("scalar", "tensor")]
             if in_range(s + 2):
                 scale_and_shift(s + 2)
-            for piece in scalar_pieces:
-                regroup_weights(piece, "scalar", 0, 2)
+            for piece, engine in scalar_pieces:
+                regroup_weights(piece, engine, 0, 2)
             if VECTOR_STATS <= s + 4 < n_groups:
                 scalar_statistics(s + 4)
-            for piece in scalar_pieces:
-                regroup_weights(piece, "scalar", 1, 2)
+            for piece, engine in scalar_pieces:
+                regroup_weights(piece, engine, 1, 2)
 
             if in_range(s + 1):
                 regroup(s + 1)

@@ -48,7 +48,7 @@ def tile_multiscalesattn_pa_kernel(
         consts = ctx.enter_context(tc.tile_pool(name="consts", bufs=1))
         small = ctx.enter_context(tc.tile_pool(name="small", bufs=8))
         scratch = ctx.enter_context(tc.tile_pool(name="scratch", bufs=2))
-        work = ctx.enter_context(tc.tile_pool(name="work", bufs=4))
+        work = ctx.enter_context(tc.tile_pool(name="work", bufs=5))
         results = ctx.enter_context(tc.tile_pool(name="results", bufs=8))
         psum_t = ctx.enter_context(tc.psum_pool(name="psum_t", bufs=4))
         psum_acc = ctx.enter_context(tc.psum_pool(name="psum_acc", bufs=4))
@@ -109,14 +109,15 @@ def tile_multiscalesattn_pa_kernel(
 
         bias_rows = consts.tile([P, n_scales * OUT_COLS], BF16)
 
-        def spread_bias(piece):
-            c, n = divmod(piece, PIECES)
-            bias_bank = psum_acc.tile([P, N_TILE], BF16, tag="acc")
-            nc.tensor.matmul(
-                out=bias_bank[:], lhsT=identity_bf16[:, c : c + 1].to_broadcast([P, P]),
-                rhs=bias_src[:, n * N_TILE : (n + 1) * N_TILE], start=True, stop=True,
-            )
-            nc.scalar.copy(out=bias_rows[:, piece * N_TILE : (piece + 1) * N_TILE], in_=bias_bank[:])
+        def spread_biases(c):
+            for n in range(PIECES):
+                bias_bank = psum_acc.tile([P, N_TILE], BF16, tag="acc")
+                nc.tensor.matmul(
+                    out=bias_bank[:], lhsT=identity_bf16[:, c : c + 1].to_broadcast([P, P]),
+                    rhs=bias_src[:, n * N_TILE : (n + 1) * N_TILE], start=True, stop=True,
+                )
+                first = c * OUT_COLS + n * N_TILE
+                nc.scalar.copy(out=bias_rows[:, first : first + N_TILE], in_=bias_bank[:])
 
         w_codes = [consts.tile([P, OUT_COLS], U32, name="w_codes%d" % c, align_bytes=64) for c in range(n_scales)]
         w_scales = [consts.tile([P, OUT_COLS], U8, name="w_scales%d" % c, align_bytes=64) for c in range(n_scales)]
@@ -163,6 +164,7 @@ def tile_multiscalesattn_pa_kernel(
         moments_of = {}
         neg_mean = {}
         rstd = {}
+        xn = {}
         xT = {}
         hT = {}
         h_grouped = {}
@@ -207,15 +209,17 @@ def tile_multiscalesattn_pa_kernel(
                 out=rstd[g][:], in_=sum_sq[:], func=ACT.Abs_reciprocal_sqrt, bias=eps[:, 0:1], scale=1.0 / FEATURES
             )
 
-        def normalise_and_transpose(g):
-            xn = work.tile([P, GROUP, FEATURES], F32)
+        def normalise(g):
+            xn[g] = work.tile([P, GROUP, FEATURES], F32, name="xn")
             for i in range(GROUP):
                 nc.gpsimd.tensor_scalar(
-                    out=xn[:, i, :].rearrange("p (j q) -> p j q", j=PACK),
+                    out=xn[g][:, i, :].rearrange("p (j q) -> p j q", j=PACK),
                     in0=x_all[:, g, i, :].rearrange("p (q j) -> p j q", j=PACK),
                     scalar1=neg_mean[g][:, i : i + 1], scalar2=rstd[g][:, i : i + 1],
                     op0=ALU.add, op1=ALU.mult,
                 )
+
+        def transpose(g):
             xT[g] = []
             for b in range(PACK // CHUNKS_PER_BANK):
                 bank = psum_t.tile([P, CHUNKS_PER_BANK, GROUP_TOKENS], F32, name="xT", tag="xT")
@@ -225,7 +229,7 @@ def tile_multiscalesattn_pa_kernel(
                     for i in range(GROUP):
                         nc.tensor.transpose(
                             out=bank[:, jj, i * P : (i + 1) * P],
-                            in_=xn[:, i, j * P : (j + 1) * P],
+                            in_=xn[g][:, i, j * P : (j + 1) * P],
                             identity=identity[:],
                         )
 
@@ -269,65 +273,56 @@ def tile_multiscalesattn_pa_kernel(
                     out=result[:, cols], in0=acc[:],
                     in1=bias_rows[:, c * OUT_COLS + n * N_TILE : c * OUT_COLS + (n + 1) * N_TILE], op=ALU.add,
                 )
-                if g == n_groups - 1 and i == GROUP - 1:
+                if g == n_groups - 1:
                     nc.sync.dma_start(out=out_groups[g, :, i, cols], in_=result[:, cols])
-            if g < n_groups - 1 or i < GROUP - 1:
+            if g < n_groups - 1:
                 nc.sync.dma_start(out=out_groups[g, :, i, :], in_=result[:])
 
-        regroup_plan = {
-            -4: ((0, "vector"),), -3: ((1, "tensor"),), -2: ((2, "tensor"),), -1: ((3, "vector"), (4, "tensor")),
-            0: ((5, "tensor"),), 1: ((6, "scalar"),), 2: ((7, "gpsimd"),), 3: ((8, "scalar"),),
-        }
+        n_pieces = n_scales * PIECES
+        regroup_engine = (
+            "tensor", "vector", "tensor", "scalar", "tensor", "scalar", "scalar", "tensor", "scalar",
+        )
 
         def in_range(g):
             return 0 <= g < n_groups
 
-        gpsimd_parts = []
-        to_quantise = []
-        for s in range(-4, n_groups + 1):
-            pieces = regroup_plan.get(s, ())
-            if s + 4 < VECTOR_STATS:
-                vector_statistics(s + 4)
-            if s == -4:
-                for piece in range(PIECES):
-                    spread_bias(piece)
-            if s + 4 < VECTOR_STATS:
-                roots(s + 4)
-            if s == -4:
-                for piece in range(PIECES, n_scales * PIECES):
-                    spread_bias(piece)
-            for piece, engine in pieces:
-                if engine == "vector":
-                    regroup_weights(piece, engine, 0, 1)
-            if in_range(s):
-                quantise(s)
-            if in_range(s - 1):
-                project(s - 1, 1)
-            if in_range(s):
-                project(s, 0)
-            for piece in to_quantise:
+        def regroup_piece(piece):
+            if 0 <= piece < n_pieces:
+                parts = 2 if regroup_engine[piece] == "tensor" else 1
+                for part in range(parts):
+                    regroup_weights(piece, regroup_engine[piece], part, parts)
+
+        def quantise_piece(piece):
+            if 0 <= piece < n_pieces:
                 quantise_weights(piece)
-            to_quantise = [piece for piece, engine in pieces if engine != "gpsimd"]
 
-            scalar_pieces = [(piece, engine) for piece, engine in pieces if engine in ("scalar", "tensor")]
-            if in_range(s + 2):
-                scale_and_shift(s + 2)
-            for piece, engine in scalar_pieces:
-                regroup_weights(piece, engine, 0, 2)
-            if VECTOR_STATS <= s + 4 < n_groups:
-                scalar_statistics(s + 4)
-            for piece, engine in scalar_pieces:
-                regroup_weights(piece, engine, 1, 2)
-
-            if in_range(s + 1):
-                regroup(s + 1)
-            gpsimd_parts += [(piece, part) for piece, engine in pieces if engine == "gpsimd" for part in range(4)]
-            for k in range(2):
-                if gpsimd_parts:
-                    piece, part = gpsimd_parts[0]
-                    gpsimd_parts = gpsimd_parts[1:]
-                    regroup_weights(piece, "gpsimd", part, 4)
-                    if part == 3:
-                        to_quantise.append(piece)
-                if k == 0 and in_range(s + 3):
-                    normalise_and_transpose(s + 3)
+        for g in range(-5, n_groups):
+            if in_range(g + 1):
+                regroup(g + 1)
+            regroup_piece(2 * g + 5)
+            if in_range(g):
+                project(g, 0)
+            quantise_piece(2 * g + 4)
+            if in_range(g + 2):
+                transpose(g + 2)
+            if in_range(g + 1):
+                quantise(g + 1)
+            if in_range(g + 2):
+                scale_and_shift(g + 2)
+            regroup_piece(2 * g + 6)
+            if in_range(g):
+                project(g, 1)
+            if g == -5:
+                spread_biases(0)
+            if VECTOR_STATS <= g + 4 < n_groups:
+                scalar_statistics(g + 4)
+            if g + 5 < VECTOR_STATS:
+                vector_statistics(g + 5)
+                roots(g + 5)
+            if g == -4:
+                spread_biases(1)
+            if g == -2:
+                spread_biases(2)
+            if in_range(g + 3):
+                normalise(g + 3)
+            quantise_piece(2 * g + 5)

@@ -18,13 +18,15 @@ FEATURES = P * PACK
 OUT_COLS = 1536
 N_TILE = 512
 PIECES = OUT_COLS // N_TILE
-SEGMENT_TOKENS = (512, 1024, 1536)
+SEGMENT_TOKENS = (1536, 1024, 512)
+SEGMENT_FIRST = (1536, 512, 0)
 EPS = 1e-5
 GROUP = 2
 GROUP_TOKENS = GROUP * P
 CHUNKS_PER_BANK = N_TILE // GROUP_TOKENS
 RUN = 4
-VECTOR_STATS = 5
+VECTOR_STATS = 6
+PROMPT_ROOTS = 2
 
 FLOPS = 2 * sum(SEGMENT_TOKENS) * FEATURES * OUT_COLS
 
@@ -33,15 +35,17 @@ def tile_multiscalesattn_pa_kernel(
     tc, x, gamma, beta, Wqkv_s, bqkv_s, Wqkv_m, bqkv_m, Wqkv_l, bqkv_l, out
 ):
     nc = tc.nc
-    weights = (Wqkv_s, Wqkv_m, Wqkv_l)
-    biases = (bqkv_s, bqkv_m, bqkv_l)
+    weights = (Wqkv_l, Wqkv_m, Wqkv_s)
+    biases = (bqkv_l, bqkv_m, bqkv_s)
     n_scales = len(weights)
 
     x_groups = x.flatten_outer_dims().rearrange("(g p i) k -> g p i k", p=P, i=GROUP)
     out_groups = out.flatten_outer_dims().rearrange("(g p i) n -> g p i n", p=P, i=GROUP)
     n_groups = sum(SEGMENT_TOKENS) // GROUP_TOKENS
-    first_group = [sum(SEGMENT_TOKENS[:c]) // GROUP_TOKENS for c in range(n_scales)]
-    scale_of_group = [max(c for c in range(n_scales) if first_group[c] <= g) for g in range(n_groups)]
+    scale_of_group = [c for c in range(n_scales) for d in range(SEGMENT_TOKENS[c] // GROUP_TOKENS)]
+    dram_group = [
+        SEGMENT_FIRST[c] // GROUP_TOKENS + d for c in range(n_scales) for d in range(SEGMENT_TOKENS[c] // GROUP_TOKENS)
+    ]
 
     with ExitStack() as ctx:
         ctx.enter_context(tc.manual_schedule())
@@ -71,9 +75,8 @@ def tile_multiscalesattn_pa_kernel(
         ]
 
         def load_x(first, last):
-            nc.sync.dma_start(
-                out=x_all[:, first : last + 1, :, :], in_=x_groups[first : last + 1].rearrange("g p i k -> p g i k")
-            )
+            rows = x_groups[dram_group[first] : dram_group[last] + 1]
+            nc.sync.dma_start(out=x_all[:, first : last + 1, :, :], in_=rows.rearrange("g p i k -> p g i k"))
 
         def load_weights(piece):
             c, n = divmod(piece, PIECES)
@@ -86,26 +89,30 @@ def tile_multiscalesattn_pa_kernel(
         load_x(0, 0)
         for c in range(n_scales):
             nc.sync.dma_start(out=bias_src[c : c + 1, :], in_=biases[c].rearrange("(o n) -> o n", o=1))
-        load_weights(0)
-        load_x(1, 1)
         nc.sync.dma_start(out=gamma_raw[:], in_=gamma.rearrange("(p j) -> p j", j=PACK))
         nc.sync.dma_start(out=beta_raw[:], in_=beta.rearrange("(p j) -> p j", j=PACK))
-        load_weights(1)
+        load_x(1, 1)
+        load_weights(0)
         load_x(2, 2)
+        load_weights(1)
         load_weights(2)
         load_x(3, 3)
+        load_x(4, 5)
         load_weights(3)
         load_weights(4)
+        load_x(6, 7)
         load_weights(5)
-        load_x(4, 5)
-        for piece in range(6, 9):
-            load_weights(piece)
-        for first in range(6, n_groups, 2):
-            load_x(first, first + 1)
+        load_weights(6)
+        load_x(8, 9)
+        load_x(10, 11)
+        load_weights(7)
+        load_weights(8)
 
         gb_cols = consts.tile([P, 2 * PACK], F32)
-        nc.gpsimd.tensor_copy(out=gb_cols[:, 0:PACK], in_=gamma_raw[:])
-        nc.gpsimd.tensor_copy(out=gb_cols[:, PACK : 2 * PACK], in_=beta_raw[:])
+
+        def convert_gamma_and_beta():
+            nc.scalar.copy(out=gb_cols[:, 0:PACK], in_=gamma_raw[:])
+            nc.scalar.copy(out=gb_cols[:, PACK : 2 * PACK], in_=beta_raw[:])
 
         bias_rows = consts.tile([P, n_scales * OUT_COLS], BF16)
 
@@ -274,55 +281,61 @@ def tile_multiscalesattn_pa_kernel(
                     in1=bias_rows[:, c * OUT_COLS + n * N_TILE : c * OUT_COLS + (n + 1) * N_TILE], op=ALU.add,
                 )
                 if g == n_groups - 1:
-                    nc.sync.dma_start(out=out_groups[g, :, i, cols], in_=result[:, cols])
+                    nc.sync.dma_start(out=out_groups[dram_group[g], :, i, cols], in_=result[:, cols])
             if g < n_groups - 1:
-                nc.sync.dma_start(out=out_groups[g, :, i, :], in_=result[:])
+                nc.sync.dma_start(out=out_groups[dram_group[g], :, i, :], in_=result[:])
 
-        n_pieces = n_scales * PIECES
-        regroup_engine = (
-            "tensor", "vector", "tensor", "scalar", "tensor", "scalar", "scalar", "tensor", "scalar",
+        regroup_step = (
+            ("vector", -3, 1), ("tensor", -2, 1), ("scalar", -2, 1),
+            ("scalar", 0, 0), ("scalar", 1, 0), ("tensor", 4, 0),
+            ("vector", 4, 0), ("scalar", 8, 0), ("scalar", 9, 1),
         )
 
         def in_range(g):
             return 0 <= g < n_groups
 
-        def regroup_piece(piece):
-            if 0 <= piece < n_pieces:
-                parts = 2 if regroup_engine[piece] == "tensor" else 1
-                for part in range(parts):
-                    regroup_weights(piece, regroup_engine[piece], part, parts)
+        def pieces_of(step, half):
+            return [piece for piece, place in enumerate(regroup_step) if place[1:] == (step, half)]
 
-        def quantise_piece(piece):
-            if 0 <= piece < n_pieces:
+        def regroup_pieces(step, half):
+            for piece in pieces_of(step, half):
+                engine = regroup_step[piece][0]
+                parts = 2 if engine == "tensor" else 1
+                for part in range(parts):
+                    regroup_weights(piece, engine, part, parts)
+
+        def quantise_pieces(step, half):
+            for piece in pieces_of(step, half):
                 quantise_weights(piece)
 
-        for g in range(-5, n_groups):
+        for g in range(-6, n_groups):
             if in_range(g + 1):
                 regroup(g + 1)
-            regroup_piece(2 * g + 5)
-            if in_range(g):
-                project(g, 0)
-            quantise_piece(2 * g + 4)
+            quantise_pieces(g - 1, 1)
             if in_range(g + 2):
                 transpose(g + 2)
+            if in_range(g):
+                project(g, 0)
             if in_range(g + 1):
                 quantise(g + 1)
+            regroup_pieces(g, 0)
             if in_range(g + 2):
                 scale_and_shift(g + 2)
-            regroup_piece(2 * g + 6)
+            if VECTOR_STATS <= g + 5 < n_groups:
+                scalar_statistics(g + 5)
+            quantise_pieces(g, 0)
+            regroup_pieces(g, 1)
+            if PROMPT_ROOTS <= g + 5 < VECTOR_STATS:
+                roots(g + 5)
             if in_range(g):
                 project(g, 1)
-            if g == -5:
-                spread_biases(0)
-            if VECTOR_STATS <= g + 4 < n_groups:
-                scalar_statistics(g + 4)
-            if g + 5 < VECTOR_STATS:
-                vector_statistics(g + 5)
-                roots(g + 5)
-            if g == -4:
-                spread_biases(1)
-            if g == -2:
-                spread_biases(2)
+            if g + 6 < VECTOR_STATS:
+                vector_statistics(g + 6)
+                if g + 6 < PROMPT_ROOTS:
+                    roots(g + 6)
+            if g + 6 < n_scales:
+                spread_biases(g + 6)
+            if g == -6:
+                convert_gamma_and_beta()
             if in_range(g + 3):
                 normalise(g + 3)
-            quantise_piece(2 * g + 5)

@@ -91,22 +91,17 @@ def tile_multiscalesattn_pa_kernel(
             nc.sync.dma_start(out=bias_src[c : c + 1, :], in_=biases[c].rearrange("(o n) -> o n", o=1))
         nc.sync.dma_start(out=gamma_raw[:], in_=gamma.rearrange("(p j) -> p j", j=PACK))
         nc.sync.dma_start(out=beta_raw[:], in_=beta.rearrange("(p j) -> p j", j=PACK))
-        load_x(1, 1)
-        load_weights(0)
-        load_x(2, 2)
-        load_weights(1)
-        load_weights(2)
-        load_x(3, 3)
+        for g in range(1, 4):
+            load_x(g, g)
+        for piece in range(3):
+            load_weights(piece)
         load_x(4, 5)
-        load_weights(3)
-        load_weights(4)
-        load_x(6, 7)
-        load_weights(5)
-        load_weights(6)
-        load_x(8, 9)
-        load_x(10, 11)
-        load_weights(7)
-        load_weights(8)
+        for piece in range(3, 7):
+            load_weights(piece)
+        for first in range(6, n_groups, 2):
+            load_x(first, first + 1)
+        for piece in range(7, 9):
+            load_weights(piece)
 
         gb_cols = consts.tile([P, 2 * PACK], F32)
 
@@ -286,56 +281,53 @@ def tile_multiscalesattn_pa_kernel(
                 nc.sync.dma_start(out=out_groups[dram_group[g], :, i, :], in_=result[:])
 
         regroup_step = (
-            ("vector", -3, 1), ("tensor", -2, 1), ("scalar", -2, 1),
-            ("scalar", 0, 0), ("scalar", 1, 0), ("tensor", 4, 0),
-            ("vector", 4, 0), ("scalar", 8, 0), ("scalar", 9, 1),
+            ("vector", -3), ("scalar", -2), ("tensor", -1),
+            ("scalar", -1), ("vector", 0), ("tensor", 0),
+            ("scalar", 0), ("scalar", 7), ("scalar", 8),
         )
+        bias_step = (-5, -4, 0)
 
         def in_range(g):
             return 0 <= g < n_groups
 
-        def pieces_of(step, half):
-            return [piece for piece, place in enumerate(regroup_step) if place[1:] == (step, half)]
+        def regroup_pieces(step, on_scalar):
+            for piece, (engine, when) in enumerate(regroup_step):
+                if when == step and (engine == "scalar") == on_scalar:
+                    parts = 2 if engine == "tensor" else 1
+                    for part in range(parts):
+                        regroup_weights(piece, engine, part, parts)
 
-        def regroup_pieces(step, half):
-            for piece in pieces_of(step, half):
-                engine = regroup_step[piece][0]
-                parts = 2 if engine == "tensor" else 1
-                for part in range(parts):
-                    regroup_weights(piece, engine, part, parts)
-
-        def quantise_pieces(step, half):
-            for piece in pieces_of(step, half):
-                quantise_weights(piece)
+        def quantise_pieces(step):
+            for piece, (engine, when) in enumerate(regroup_step):
+                if step == (when + 1 if engine == "scalar" else when):
+                    quantise_weights(piece)
 
         for g in range(-6, n_groups):
-            if in_range(g + 1):
-                regroup(g + 1)
-            quantise_pieces(g - 1, 1)
-            if in_range(g + 2):
-                transpose(g + 2)
+            if VECTOR_STATS <= g + 4 < n_groups:
+                scalar_statistics(g + 4)
             if in_range(g):
                 project(g, 0)
+            regroup_pieces(g, False)
+            if g in bias_step:
+                spread_biases(bias_step.index(g))
+            if g == -5:
+                convert_gamma_and_beta()
+            if in_range(g + 2):
+                transpose(g + 2)
+                scale_and_shift(g + 2)
+            if in_range(g + 1):
+                regroup(g + 1)
+            regroup_pieces(g, True)
             if in_range(g + 1):
                 quantise(g + 1)
-            regroup_pieces(g, 0)
-            if in_range(g + 2):
-                scale_and_shift(g + 2)
-            if VECTOR_STATS <= g + 5 < n_groups:
-                scalar_statistics(g + 5)
-            quantise_pieces(g, 0)
-            regroup_pieces(g, 1)
+            quantise_pieces(g)
             if PROMPT_ROOTS <= g + 5 < VECTOR_STATS:
                 roots(g + 5)
             if in_range(g):
                 project(g, 1)
+            if in_range(g + 3):
+                normalise(g + 3)
             if g + 6 < VECTOR_STATS:
                 vector_statistics(g + 6)
                 if g + 6 < PROMPT_ROOTS:
                     roots(g + 6)
-            if g + 6 < n_scales:
-                spread_biases(g + 6)
-            if g == -6:
-                convert_gamma_and_beta()
-            if in_range(g + 3):
-                normalise(g + 3)

@@ -272,8 +272,8 @@ def tile_multiscalesattn_pa_kernel(
                     start=True, stop=True,
                 )
                 nc.vector.tensor_tensor(
-                    out=result[:, cols], in0=acc[:],
-                    in1=bias_rows[:, c * OUT_COLS + n * N_TILE : c * OUT_COLS + (n + 1) * N_TILE], op=ALU.add,
+                    out=result[:, cols], in0=bias_rows[:, c * OUT_COLS + n * N_TILE : c * OUT_COLS + (n + 1) * N_TILE],
+                    in1=acc[:], op=ALU.add,
                 )
                 if g == n_groups - 1:
                     nc.sync.dma_start(out=out_groups[dram_group[g], :, i, cols], in_=result[:, cols])

from contextlib import ExitStack

import concourse.mybir as mybir
from concourse.masks import make_identity

F32 = mybir.dt.float32
BF16 = mybir.dt.bfloat16
I32 = mybir.dt.int32
U32 = mybir.dt.uint32
U8 = mybir.dt.uint8
FP8X4 = mybir.dt.float8_e4m3fn_x4
ACT = mybir.ActivationFunctionType
ALU = mybir.AluOpType

P = 128
PACK = 4
FEATURES = P * PACK
OUT_COLS = 1536
N_TILE = 512
PIECES = OUT_COLS // N_TILE
SEGMENT_TOKENS = (1536, 1024, 512)
SEGMENT_FIRST = (1536, 512, 0)
EPS = 1e-5
GROUP = 2
GROUP_TOKENS = GROUP * P
CHUNKS_PER_BANK = N_TILE // GROUP_TOKENS
RUN = 4
VECTOR_STATS = 6
PROMPT_ROOTS = 2

FLOPS = 2 * sum(SEGMENT_TOKENS) * FEATURES * OUT_COLS


def tile_multiscalesattn_pa_kernel(
    tc, x, gamma, beta, Wqkv_s, bqkv_s, Wqkv_m, bqkv_m, Wqkv_l, bqkv_l, out
):
    nc = tc.nc
    weights = (Wqkv_l, Wqkv_m, Wqkv_s)
    biases = (bqkv_l, bqkv_m, bqkv_s)
    n_scales = len(weights)

    x_groups = x.flatten_outer_dims().rearrange("(g p i) k -> g p i k", p=P, i=GROUP)
    out_groups = out.flatten_outer_dims().rearrange("(g p i) n -> g p i n", p=P, i=GROUP)
    n_groups = sum(SEGMENT_TOKENS) // GROUP_TOKENS
    scale_of_group = [c for c in range(n_scales) for d in range(SEGMENT_TOKENS[c] // GROUP_TOKENS)]
    dram_group = [
        SEGMENT_FIRST[c] // GROUP_TOKENS + d for c in range(n_scales) for d in range(SEGMENT_TOKENS[c] // GROUP_TOKENS)
    ]

    with ExitStack() as ctx:
        ctx.enter_context(tc.manual_schedule())
        consts = ctx.enter_context(tc.tile_pool(name="consts", bufs=1))
        small = ctx.enter_context(tc.tile_pool(name="small", bufs=8))
        scratch = ctx.enter_context(tc.tile_pool(name="scratch", bufs=2))
        work = ctx.enter_context(tc.tile_pool(name="work", bufs=5))
        results = ctx.enter_context(tc.tile_pool(name="results", bufs=8))
        psum_t = ctx.enter_context(tc.psum_pool(name="psum_t", bufs=4))
        psum_acc = ctx.enter_context(tc.psum_pool(name="psum_acc", bufs=4))

        bias_src = consts.tile([P, OUT_COLS], BF16)
        nc.vector.memset(bias_src[:].bitcast(I32), 0)
        eps = consts.tile([P, 1], F32)
        nc.vector.memset(eps[:], EPS)
        root_eps = consts.tile([P, 1], F32)
        nc.scalar.activation(out=root_eps[:], in_=eps[:], func=ACT.Abs_reciprocal_sqrt)
        identity = consts.tile([P, P], F32)
        make_identity(nc, identity[:])
        identity_bf16 = consts.tile([P, P], BF16)
        nc.gpsimd.tensor_copy(out=identity_bf16[:], in_=identity[:])

        x_all = consts.tile([P, n_groups, GROUP, FEATURES], BF16)
        w_raw = [
            [consts.tile([P, PACK, N_TILE], BF16, name="w_raw%d_%d" % (c, n)) for n in range(PIECES)]
            for c in range(n_scales)
        ]

        def load_x(first, last):
            rows = x_groups[dram_group[first] : dram_group[last] + 1]
            nc.sync.dma_start(out=x_all[:, first : last + 1, :, :], in_=rows.rearrange("g p i k -> p g i k"))

        def load_weights(piece):
            c, n = divmod(piece, PIECES)
            rows = weights[c].rearrange("(p j) n -> p j n", j=PACK)
            nc.sync.dma_start(out=w_raw[c][n][:], in_=rows[:, :, n * N_TILE : (n + 1) * N_TILE])

        gamma_raw = consts.tile([P, PACK], BF16)
        beta_raw = consts.tile([P, PACK], BF16)

        load_x(0, 0)
        for c in range(n_scales):
            nc.sync.dma_start(out=bias_src[c : c + 1, :], in_=biases[c].rearrange("(o n) -> o n", o=1))
        nc.sync.dma_start(out=gamma_raw[:], in_=gamma.rearrange("(p j) -> p j", j=PACK))
        nc.sync.dma_start(out=beta_raw[:], in_=beta.rearrange("(p j) -> p j", j=PACK))
        for g in range(1, 4):
            load_x(g, g)
        for piece in range(3):
            load_weights(piece)
        load_x(4, 5)
        for piece in range(3, 7):
            load_weights(piece)
        for first in range(6, n_groups, 2):
            load_x(first, first + 1)
        for piece in range(7, 9):
            load_weights(piece)

        gb_cols = consts.tile([P, 2 * PACK], F32)

        def convert_gamma_and_beta():
            nc.scalar.copy(out=gb_cols[:, 0:PACK], in_=gamma_raw[:])
            nc.scalar.copy(out=gb_cols[:, PACK : 2 * PACK], in_=beta_raw[:])

        bias_rows = consts.tile([P, n_scales * OUT_COLS], BF16)

        def spread_biases(c):
            for n in range(PIECES):
                bias_bank = psum_acc.tile([P, N_TILE], BF16, tag="acc")
                nc.tensor.matmul(
                    out=bias_bank[:], lhsT=identity_bf16[:, c : c + 1].to_broadcast([P, P]),
                    rhs=bias_src[:, n * N_TILE : (n + 1) * N_TILE], start=True, stop=True,
                )
                first = c * OUT_COLS + n * N_TILE
                nc.scalar.copy(out=bias_rows[:, first : first + N_TILE], in_=bias_bank[:])

        w_codes = [consts.tile([P, OUT_COLS], U32, name="w_codes%d" % c, align_bytes=64) for c in range(n_scales)]
        w_scales = [consts.tile([P, OUT_COLS], U8, name="w_scales%d" % c, align_bytes=64) for c in range(n_scales)]
        w_grouped = {}

        def regroup_weights(piece, engine, part, parts):
            c, n = divmod(piece, PIECES)
            if part == 0:
                w_grouped[piece] = work.tile([P, N_TILE, PACK], BF16, name="w_grouped", align_bytes=64)
            cols = slice(part * N_TILE // parts, (part + 1) * N_TILE // parts)
            dst = w_grouped[piece][:, cols, :]
            src = w_raw[c][n][:, :, cols]
            if engine == "tensor":
                bank = psum_t.tile([P, 2 * N_TILE], BF16, name="xT", tag="xT")
                width = N_TILE // PACK
                for half in range(2):
                    nc.tensor.matmul(
                        out=bank[:, half * N_TILE : (half + 1) * N_TILE], lhsT=identity_bf16[:],
                        rhs=src[:, :, half * width : (half + 1) * width].rearrange("p j w -> p w j"),
                        start=True, stop=True,
                    )
                nc.scalar.copy(out=dst.rearrange("p w j -> p (w j)"), in_=bank[:])
            elif engine == "gpsimd":
                nc.gpsimd.tensor_scalar(
                    out=dst, in0=src.rearrange("p j w -> p w j"), scalar1=1.0, scalar2=0.0, op0=ALU.mult, op1=ALU.add
                )
            else:
                dst_runs = dst.rearrange("p (w r) j -> p w j r", r=RUN)
                src_runs = src.rearrange("p j (w r) -> p w j r", r=RUN)
                if engine == "vector":
                    nc.vector.tensor_copy(out=dst_runs, in_=src_runs)
                else:
                    nc.scalar.copy(out=dst_runs, in_=src_runs)

        def quantise_weights(piece):
            c, n = divmod(piece, PIECES)
            cols = slice(n * N_TILE, (n + 1) * N_TILE)
            nc.vector.quantize_mx(
                out=w_codes[c][:, cols].bitcast(FP8X4),
                scales=w_scales[c][:, cols],
                in_=w_grouped[piece][:].rearrange("p w j -> p (w j)"),
            )

        moments_of = {}
        neg_mean = {}
        rstd = {}
        xn = {}
        xT = {}
        hT = {}
        h_grouped = {}
        h_codes = {}
        h_scales = {}

        def vector_statistics(g):
            moments = small.tile([P, GROUP, 2], F32)
            partial = small.tile([P, GROUP, 6], F32)
            for i in range(GROUP):
                nc.vector.bn_stats(out=partial[:, i, :], in_=x_all[:, g, i, :])
            for i in range(GROUP):
                nc.vector.bn_aggr(out=moments[:, i, :], in_=partial[:, i, :])
            moments_of[g] = moments

        def roots(g):
            moments = moments_of[g]
            neg_mean[g] = small.tile([P, GROUP], F32, name="neg_mean")
            nc.scalar.activation(out=neg_mean[g][:], in_=moments[:, :, 0], func=ACT.Copy, scale=-1.0)
            rstd[g] = small.tile([P, GROUP], F32, name="rstd")
            nc.scalar.activation(
                out=rstd[g][:], in_=moments[:, :, 1], func=ACT.Abs_reciprocal_sqrt, bias=eps[:, 0:1], scale=1.0
            )

        def scalar_statistics(g):
            neg_mean[g] = small.tile([P, GROUP], F32, name="neg_mean")
            sum_sq = small.tile([P, GROUP], F32)
            for i in range(GROUP):
                unread = scratch.tile([P, FEATURES], BF16)
                nc.scalar.activation(
                    out=unread[:], in_=x_all[:, g, i, :], func=ACT.Copy, scale=-1.0 / FEATURES,
                    accum_out=neg_mean[g][:, i : i + 1],
                )
            for i in range(GROUP):
                unread = scratch.tile([P, FEATURES], BF16)
                nc.scalar.activation(
                    out=unread[:], in_=x_all[:, g, i, :], func=ACT.Square,
                    bias=neg_mean[g][:, i : i + 1], scale=1.0, accum_out=sum_sq[:, i : i + 1],
                )
            rstd[g] = small.tile([P, GROUP], F32, name="rstd")
            nc.scalar.activation(
                out=rstd[g][:], in_=sum_sq[:], func=ACT.Abs_reciprocal_sqrt, bias=eps[:, 0:1], scale=1.0 / FEATURES
            )

        def normalise(g):
            xn[g] = work.tile([P, GROUP, FEATURES], F32, name="xn")
            for i in range(GROUP):
                nc.gpsimd.tensor_scalar(
                    out=xn[g][:, i, :].rearrange("p (j q) -> p j q", j=PACK),
                    in0=x_all[:, g, i, :].rearrange("p (q j) -> p j q", j=PACK),
                    scalar1=neg_mean[g][:, i : i + 1], scalar2=rstd[g][:, i : i + 1],
                    op0=ALU.add, op1=ALU.mult,
                )

        def transpose(g):
            xT[g] = []
            for b in range(PACK // CHUNKS_PER_BANK):
                bank = psum_t.tile([P, CHUNKS_PER_BANK, GROUP_TOKENS], F32, name="xT", tag="xT")
                xT[g].append(bank)
                for jj in range(CHUNKS_PER_BANK):
                    j = b * CHUNKS_PER_BANK + jj
                    for i in range(GROUP):
                        nc.tensor.transpose(
                            out=bank[:, jj, i * P : (i + 1) * P],
                            in_=xn[g][:, i, j * P : (j + 1) * P],
                            identity=identity[:],
                        )

        def scale_and_shift(g):
            hT[g] = work.tile([P, PACK, GROUP_TOKENS], BF16, name="hT")
            for j in range(PACK):
                nc.scalar.activation(
                    out=hT[g][:, j, :], in_=xT[g][j // CHUNKS_PER_BANK][:, j % CHUNKS_PER_BANK, :],
                    func=ACT.Identity, scale=gb_cols[:, j : j + 1], bias=gb_cols[:, PACK + j : PACK + j + 1],
                )

        def regroup(g):
            h_grouped[g] = work.tile([P, GROUP_TOKENS, PACK], BF16, name="h_grouped", align_bytes=64)
            nc.gpsimd.tensor_scalar(
                out=h_grouped[g][:], in0=hT[g][:].rearrange("p j w -> p w j"),
                scalar1=1.0, scalar2=0.0, op0=ALU.mult, op1=ALU.add,
            )

        def quantise(g):
            h_codes[g] = work.tile([P, GROUP_TOKENS], U32, name="h_codes", align_bytes=64)
            h_scales[g] = work.tile([P, GROUP_TOKENS], U8, name="h_scales", align_bytes=64)
            nc.vector.quantize_mx(
                out=h_codes[g][:].bitcast(FP8X4), scales=h_scales[g][:],
                in_=h_grouped[g][:].rearrange("p w j -> p (w j)"),
            )

        def project(g, i):
            c = scale_of_group[g]
            tokens = slice(i * P, (i + 1) * P)
            result = results.tile([P, OUT_COLS], F32)
            for n in range(PIECES):
                cols = slice(n * N_TILE, (n + 1) * N_TILE)
                acc = psum_acc.tile([P, N_TILE], F32, tag="acc")
                nc.tensor.matmul_mx(
                    out=acc[:],
                    lhsT=h_codes[g][:, tokens].bitcast(FP8X4), lhsT_scale=h_scales[g][:, tokens],
                    rhs=w_codes[c][:, cols].bitcast(FP8X4), rhs_scale=w_scales[c][:, cols],
                    start=True, stop=True,
                )
                nc.vector.tensor_tensor(
                    out=result[:, cols], in0=bias_rows[:, c * OUT_COLS + n * N_TILE : c * OUT_COLS + (n + 1) * N_TILE],
                    in1=acc[:], op=ALU.add,
                )
                if g == n_groups - 1:
                    nc.sync.dma_start(out=out_groups[dram_group[g], :, i, cols], in_=result[:, cols])
            if g < n_groups - 1:
                nc.sync.dma_start(out=out_groups[dram_group[g], :, i, :], in_=result[:])

        regroup_step = (
            ("vector", -3), ("scalar", -2), ("tensor", -1),
            ("scalar", -1), ("vector", 0), ("tensor", 0),
            ("scalar", 0), ("scalar", 7), ("scalar", 8),
        )
        bias_step = (-5, -4, 0)

        def in_range(g):
            return 0 <= g < n_groups

        def regroup_pieces(step, on_scalar):
            for piece, (engine, when) in enumerate(regroup_step):
                if when == step and (engine == "scalar") == on_scalar:
                    parts = 2 if engine == "tensor" else 1
                    for part in range(parts):
                        regroup_weights(piece, engine, part, parts)

        def quantise_pieces(step):
            for piece, (engine, when) in enumerate(regroup_step):
                if step == (when + 1 if engine == "scalar" else when):
                    quantise_weights(piece)

        for g in range(-6, n_groups):
            if VECTOR_STATS <= g + 4 < n_groups:
                scalar_statistics(g + 4)
            if in_range(g):
                project(g, 0)
            regroup_pieces(g, False)
            if g in bias_step:
                spread_biases(bias_step.index(g))
            if g == -5:
                convert_gamma_and_beta()
            if in_range(g + 2):
                transpose(g + 2)
                scale_and_shift(g + 2)
            if in_range(g + 1):
                regroup(g + 1)
            regroup_pieces(g, True)
            if in_range(g + 1):
                quantise(g + 1)
            quantise_pieces(g)
            if PROMPT_ROOTS <= g + 5 < VECTOR_STATS:
                roots(g + 5)
            if in_range(g):
                project(g, 1)
            if in_range(g + 3):
                normalise(g + 3)
            if g + 6 < VECTOR_STATS:
                vector_statistics(g + 6)
                if g + 6 < PROMPT_ROOTS:
                    roots(g + 6)
